import numpy as np
import ml_dtypes

BF16 = ml_dtypes.bfloat16


def bf(x):
    return np.asarray(x, np.float32).astype(BF16)


def f32(x):
    return np.asarray(x, np.float32)


def f64(x):
    return np.asarray(x).astype(np.float64)


def striped(idx):
    return np.tile(idx.reshape(-1, 16).T, (8, 1))


D, S, N = 128, 1024, 512


def setup_inputs():
    return {"x": f32(bf(np.random.standard_normal((D, S)))), "w": bf(np.random.standard_normal((D, D)) / np.sqrt(D)), "adj_t": bf(np.random.uniform(size=(N, N)) * 2.0 / np.sqrt(N)), "b": f32(0.1 * np.random.standard_normal((D, 1))), "offs": striped(np.random.permutation(S)[:N])}


def reference(x, w, adj_t, b, offs):
    idx = offs[:16].T.reshape(-1)
    y = f64(x)[:, idx].T @ f64(w)
    return np.maximum(y.T @ f64(adj_t) + f64(b), 0.0)

@@ -1,0 +1,47 @@
+import concourse.mybir as mybir
+
+F32, BF16, U16 = mybir.dt.float32, mybir.dt.bfloat16, mybir.dt.uint16
+COPY = mybir.ActivationFunctionType.Copy
+ADD, MAX = mybir.AluOpType.add, mybir.AluOpType.max
+
+P = 128
+NODES = 1024
+PICKED = 512
+BLOCKS = PICKED // P
+
+FLOPS = 2 * PICKED * P * P + 2 * PICKED * PICKED * P
+
+
+def tile_fuselayer_kernel(tc, x, w, adj_t, b, offs, out):
+    nc = tc.nc
+    with (
+        tc.tile_pool(name="held", bufs=1) as held,
+        tc.psum_pool(name="psum", bufs=1) as psum,
+    ):
+        offsets = held.tile([P, PICKED // 16], U16, name="offsets")
+        nc.sync.dma_start(offsets[:], offs)
+        nodes = held.tile([P, NODES], F32, name="nodes")
+        nc.sync.dma_start(nodes[:], x)
+        weights = held.tile([P, P], BF16, name="weights")
+        nc.scalar.dma_start(weights[:], w)
+        adjacency = held.tile([P, BLOCKS, PICKED], BF16, name="adjacency")
+        nc.sync.dma_start(adjacency[:], adj_t.rearrange("(k p) i -> p k i", p=P))
+        bias = held.tile([P, 1], F32, name="bias")
+        nc.scalar.dma_start(bias[:], b)
+
+        picked = held.tile([P, PICKED], F32, name="picked")
+        nc.scalar.activation(picked[:], nodes[:].indirect(offsets[:]), COPY)
+        picked_bf = held.tile([P, PICKED], BF16, name="picked_bf")
+        nc.vector.tensor_copy(picked_bf[:], picked[:])
+
+        total = psum.tile([P, PICKED], F32, name="total")
+        for k in range(BLOCKS):
+            projected = psum.tile([P, P], F32, name=f"projected{k}")
+            nc.tensor.matmul(projected[:], picked_bf[:, k * P : (k + 1) * P], weights[:], start=True, stop=True)
+            rounded = held.tile([P, P], BF16, name=f"rounded{k}")
+            nc.vector.tensor_copy(rounded[:], projected[:])
+            nc.tensor.matmul(total[:], rounded[:], adjacency[:, k, :], start=(k == 0), stop=(k == BLOCKS - 1))
+
+        result = held.tile([P, PICKED], F32, name="result")
+        nc.vector.tensor_scalar(result[:], total[:], bias[:, 0:1], 0.0, ADD, MAX)
+        nc.sync.dma_start(out, result[:])

@@ -23,11 +23,15 @@ def tile_fuselayer_kernel(tc, x, w, adj_t, b, offs, out):
         nodes = held.tile([P, NODES], F32, name="nodes")
         nc.sync.dma_start(nodes[:], x)
         weights = held.tile([P, P], BF16, name="weights")
-        nc.scalar.dma_start(weights[:], w)
+        nc.sync.dma_start(weights[:], w)
         adjacency = held.tile([P, BLOCKS, PICKED], BF16, name="adjacency")
         nc.sync.dma_start(adjacency[:], adj_t.rearrange("(k p) i -> p k i", p=P))
         bias = held.tile([P, 1], F32, name="bias")
-        nc.scalar.dma_start(bias[:], b)
+        nc.sync.dma_start(bias[:], b)
+
+        first = held.tile([P, 1], F32, name="first")
+        nc.vector.memset(first[:], 0.0)
+        nc.scalar.activation(first[:], first[:], COPY)
 
         picked = held.tile([P, PICKED], F32, name="picked")
         nc.scalar.activation(picked[:], nodes[:].indirect(offsets[:]), COPY)

@@ -33,15 +33,15 @@ def tile_fuselayer_kernel(tc, x, w, adj_t, b, offs, out):
         nc.vector.memset(first[:], 0.0)
         nc.scalar.activation(first[:], first[:], COPY)
 
-        picked = held.tile([P, PICKED], F32, name="picked")
-        nc.scalar.activation(picked[:], nodes[:].indirect(offsets[:]), COPY)
-        picked_bf = held.tile([P, PICKED], BF16, name="picked_bf")
-        nc.vector.tensor_copy(picked_bf[:], picked[:])
-
         total = psum.tile([P, PICKED], F32, name="total")
         for k in range(BLOCKS):
+            picked = held.tile([P, P], F32, name=f"picked{k}")
+            block_offsets = offsets[:, k * (P // 16) : (k + 1) * (P // 16)]
+            nc.scalar.activation(picked[:], nodes[:].indirect(block_offsets), COPY)
+            picked_bf = held.tile([P, P], BF16, name=f"picked_bf{k}")
+            nc.vector.tensor_copy(picked_bf[:], picked[:])
             projected = psum.tile([P, P], F32, name=f"projected{k}")
-            nc.tensor.matmul(projected[:], picked_bf[:, k * P : (k + 1) * P], weights[:], start=True, stop=True)
+            nc.tensor.matmul(projected[:], picked_bf[:], weights[:], start=True, stop=True)
             rounded = held.tile([P, P], BF16, name=f"rounded{k}")
             nc.vector.tensor_copy(rounded[:], projected[:])
             nc.tensor.matmul(total[:], rounded[:], adjacency[:, k, :], start=(k == 0), stop=(k == BLOCKS - 1))

@@ -9,6 +9,8 @@ NODES = 1024
 PICKED = 512
 BLOCKS = PICKED // P
 
+WARM_UP = 8
+
 FLOPS = 2 * PICKED * P * P + 2 * PICKED * PICKED * P
 
 
@@ -32,6 +34,12 @@ def tile_fuselayer_kernel(tc, x, w, adj_t, b, offs, out):
         first = held.tile([P, 1], F32, name="first")
         nc.vector.memset(first[:], 0.0)
         nc.scalar.activation(first[:], first[:], COPY)
+
+        zeros = held.tile([P, PICKED], BF16, name="zeros")
+        nc.vector.memset(zeros[:], 0.0)
+        unread = psum.tile([P, PICKED], F32, name="unread")
+        for turn in range(WARM_UP):
+            nc.tensor.matmul(unread[:], zeros[:, 0:P], zeros[:], start=True, stop=True)
 
         total = psum.tile([P, PICKED], F32, name="total")
         for k in range(BLOCKS):

@@ -1,13 +1,14 @@
 import concourse.mybir as mybir
 
 F32, BF16, U16 = mybir.dt.float32, mybir.dt.bfloat16, mybir.dt.uint16
-COPY = mybir.ActivationFunctionType.Copy
+COPY, RELU = mybir.ActivationFunctionType.Copy, mybir.ActivationFunctionType.Relu
 ADD, MAX = mybir.AluOpType.add, mybir.AluOpType.max
 
 P = 128
 NODES = 1024
 PICKED = 512
 BLOCKS = PICKED // P
+HALF = PICKED // 2
 
 WARM_UP = 8
 
@@ -41,7 +42,7 @@ def tile_fuselayer_kernel(tc, x, w, adj_t, b, offs, out):
         for turn in range(WARM_UP):
             nc.tensor.matmul(unread[:], zeros[:, 0:P], zeros[:], start=True, stop=True)
 
-        total = psum.tile([P, PICKED], F32, name="total")
+        totals = [psum.tile([P, HALF], F32, name=f"total{h}") for h in range(2)]
         for k in range(BLOCKS):
             picked = held.tile([P, P], F32, name=f"picked{k}")
             block_offsets = offsets[:, k * (P // 16) : (k + 1) * (P // 16)]
@@ -52,8 +53,18 @@ def tile_fuselayer_kernel(tc, x, w, adj_t, b, offs, out):
             nc.tensor.matmul(projected[:], picked_bf[:], weights[:], start=True, stop=True)
             rounded = held.tile([P, P], BF16, name=f"rounded{k}")
             nc.vector.tensor_copy(rounded[:], projected[:])
-            nc.tensor.matmul(total[:], rounded[:], adjacency[:, k, :], start=(k == 0), stop=(k == BLOCKS - 1))
+            for h in range(2):
+                nc.tensor.matmul(
+                    totals[h][:],
+                    rounded[:],
+                    adjacency[:, k, h * HALF : (h + 1) * HALF],
+                    start=(k == 0),
+                    stop=(k == BLOCKS - 1),
+                )
 
-        result = held.tile([P, PICKED], F32, name="result")
-        nc.vector.tensor_scalar(result[:], total[:], bias[:, 0:1], 0.0, ADD, MAX)
-        nc.sync.dma_start(out, result[:])
+        result0 = held.tile([P, HALF], F32, name="result0")
+        nc.vector.tensor_scalar(result0[:], totals[0][:], bias[:, 0:1], 0.0, ADD, MAX)
+        nc.sync.dma_start(out[:, 0:HALF], result0[:])
+        result1 = held.tile([P, HALF], F32, name="result1")
+        nc.scalar.activation(result1[:], totals[1][:], RELU, bias=bias[:, 0:1])
+        nc.scalar.dma_start(out[:, HALF:PICKED], result1[:])

@@ -1,16 +1,17 @@
 import concourse.mybir as mybir
 
 F32, BF16, U16 = mybir.dt.float32, mybir.dt.bfloat16, mybir.dt.uint16
-COPY, RELU = mybir.ActivationFunctionType.Copy, mybir.ActivationFunctionType.Relu
+COPY = mybir.ActivationFunctionType.Copy
 ADD, MAX = mybir.AluOpType.add, mybir.AluOpType.max
 
 P = 128
 NODES = 1024
 PICKED = 512
 BLOCKS = PICKED // P
-HALF = PICKED // 2
 
 WARM_UP = 8
+
+X_PARTS = 4
 
 FLOPS = 2 * PICKED * P * P + 2 * PICKED * PICKED * P
 
@@ -24,7 +25,10 @@ def tile_fuselayer_kernel(tc, x, w, adj_t, b, offs, out):
         offsets = held.tile([P, PICKED // 16], U16, name="offsets")
         nc.sync.dma_start(offsets[:], offs)
         nodes = held.tile([P, NODES], F32, name="nodes")
-        nc.sync.dma_start(nodes[:], x)
+        part = NODES // X_PARTS
+        for q in range(X_PARTS):
+            queue = nc.sync if q % 2 == 0 else nc.scalar
+            queue.dma_start(nodes[:, q * part : (q + 1) * part], x[:, q * part : (q + 1) * part])
         weights = held.tile([P, P], BF16, name="weights")
         nc.sync.dma_start(weights[:], w)
         adjacency = held.tile([P, BLOCKS, PICKED], BF16, name="adjacency")
@@ -42,7 +46,7 @@ def tile_fuselayer_kernel(tc, x, w, adj_t, b, offs, out):
         for turn in range(WARM_UP):
             nc.tensor.matmul(unread[:], zeros[:, 0:P], zeros[:], start=True, stop=True)
 
-        totals = [psum.tile([P, HALF], F32, name=f"total{h}") for h in range(2)]
+        total = psum.tile([P, PICKED], F32, name="total")
         for k in range(BLOCKS):
             picked = held.tile([P, P], F32, name=f"picked{k}")
             block_offsets = offsets[:, k * (P // 16) : (k + 1) * (P // 16)]
@@ -53,18 +57,8 @@ def tile_fuselayer_kernel(tc, x, w, adj_t, b, offs, out):
             nc.tensor.matmul(projected[:], picked_bf[:], weights[:], start=True, stop=True)
             rounded = held.tile([P, P], BF16, name=f"rounded{k}")
             nc.vector.tensor_copy(rounded[:], projected[:])
-            for h in range(2):
-                nc.tensor.matmul(
-                    totals[h][:],
-                    rounded[:],
-                    adjacency[:, k, h * HALF : (h + 1) * HALF],
-                    start=(k == 0),
-                    stop=(k == BLOCKS - 1),
-                )
+            nc.tensor.matmul(total[:], rounded[:], adjacency[:, k, :], start=(k == 0), stop=(k == BLOCKS - 1))
 
-        result0 = held.tile([P, HALF], F32, name="result0")
-        nc.vector.tensor_scalar(result0[:], totals[0][:], bias[:, 0:1], 0.0, ADD, MAX)
-        nc.sync.dma_start(out[:, 0:HALF], result0[:])
-        result1 = held.tile([P, HALF], F32, name="result1")
-        nc.scalar.activation(result1[:], totals[1][:], RELU, bias=bias[:, 0:1])
-        nc.scalar.dma_start(out[:, HALF:PICKED], result1[:])
+        result = held.tile([P, PICKED], F32, name="result")
+        nc.vector.tensor_scalar(result[:], total[:], bias[:, 0:1], 0.0, ADD, MAX)
+        nc.sync.dma_start(out, result[:])

@@ -1,17 +1,16 @@
 import concourse.mybir as mybir
 
 F32, BF16, U16 = mybir.dt.float32, mybir.dt.bfloat16, mybir.dt.uint16
-COPY = mybir.ActivationFunctionType.Copy
+COPY, RELU = mybir.ActivationFunctionType.Copy, mybir.ActivationFunctionType.Relu
 ADD, MAX = mybir.AluOpType.add, mybir.AluOpType.max
 
 P = 128
 NODES = 1024
 PICKED = 512
 BLOCKS = PICKED // P
+HALF = PICKED // 2
 
 WARM_UP = 8
-
-X_PARTS = 4
 
 FLOPS = 2 * PICKED * P * P + 2 * PICKED * PICKED * P
 
@@ -25,10 +24,7 @@ def tile_fuselayer_kernel(tc, x, w, adj_t, b, offs, out):
         offsets = held.tile([P, PICKED // 16], U16, name="offsets")
         nc.sync.dma_start(offsets[:], offs)
         nodes = held.tile([P, NODES], F32, name="nodes")
-        part = NODES // X_PARTS
-        for q in range(X_PARTS):
-            queue = nc.sync if q % 2 == 0 else nc.scalar
-            queue.dma_start(nodes[:, q * part : (q + 1) * part], x[:, q * part : (q + 1) * part])
+        nc.sync.dma_start(nodes[:], x)
         weights = held.tile([P, P], BF16, name="weights")
         nc.sync.dma_start(weights[:], w)
         adjacency = held.tile([P, BLOCKS, PICKED], BF16, name="adjacency")
@@ -46,7 +42,7 @@ def tile_fuselayer_kernel(tc, x, w, adj_t, b, offs, out):
         for turn in range(WARM_UP):
             nc.tensor.matmul(unread[:], zeros[:, 0:P], zeros[:], start=True, stop=True)
 
-        total = psum.tile([P, PICKED], F32, name="total")
+        totals = [psum.tile([P, HALF], F32, name=f"total{h}") for h in range(2)]
         for k in range(BLOCKS):
             picked = held.tile([P, P], F32, name=f"picked{k}")
             block_offsets = offsets[:, k * (P // 16) : (k + 1) * (P // 16)]
@@ -57,8 +53,16 @@ def tile_fuselayer_kernel(tc, x, w, adj_t, b, offs, out):
             nc.tensor.matmul(projected[:], picked_bf[:], weights[:], start=True, stop=True)
             rounded = held.tile([P, P], BF16, name=f"rounded{k}")
             nc.vector.tensor_copy(rounded[:], projected[:])
-            nc.tensor.matmul(total[:], rounded[:], adjacency[:, k, :], start=(k == 0), stop=(k == BLOCKS - 1))
+            for h in range(2):
+                nc.tensor.matmul(
+                    totals[h][:],
+                    rounded[:],
+                    adjacency[:, k, h * HALF : (h + 1) * HALF],
+                    start=(k == 0),
+                    stop=(k == BLOCKS - 1),
+                )
 
         result = held.tile([P, PICKED], F32, name="result")
-        nc.vector.tensor_scalar(result[:], total[:], bias[:, 0:1], 0.0, ADD, MAX)
+        nc.scalar.activation(result[:, 0:HALF], totals[0][:], RELU, bias=bias[:, 0:1])
+        nc.vector.tensor_scalar(result[:, HALF:PICKED], totals[1][:], bias[:, 0:1], 0.0, ADD, MAX)
         nc.sync.dma_start(out, result[:])

@@ -47,10 +47,9 @@ def tile_fuselayer_kernel(tc, x, w, adj_t, b, offs, out):
             picked = held.tile([P, P], F32, name=f"picked{k}")
             block_offsets = offsets[:, k * (P // 16) : (k + 1) * (P // 16)]
             nc.scalar.activation(picked[:], nodes[:].indirect(block_offsets), COPY)
-            picked_bf = held.tile([P, P], BF16, name=f"picked_bf{k}")
-            nc.vector.tensor_copy(picked_bf[:], picked[:])
+            picked_bf = picked[:].bitcast(BF16)[:, 1 : 2 * P : 2]
             projected = psum.tile([P, P], F32, name=f"projected{k}")
-            nc.tensor.matmul(projected[:], picked_bf[:], weights[:], start=True, stop=True)
+            nc.tensor.matmul(projected[:], picked_bf, weights[:], start=True, stop=True)
             rounded = held.tile([P, P], BF16, name=f"rounded{k}")
             nc.vector.tensor_copy(rounded[:], projected[:])
             for h in range(2):

@@ -21,14 +21,14 @@ def tile_fuselayer_kernel(tc, x, w, adj_t, b, offs, out):
         tc.tile_pool(name="held", bufs=1) as held,
         tc.psum_pool(name="psum", bufs=1) as psum,
     ):
+        nodes = held.tile([P, NODES], F32, name="nodes")
+        nc.scalar.dma_start(nodes[:], x)
         offsets = held.tile([P, PICKED // 16], U16, name="offsets")
         nc.sync.dma_start(offsets[:], offs)
-        nodes = held.tile([P, NODES], F32, name="nodes")
-        nc.sync.dma_start(nodes[:], x)
+        adjacency = held.tile([P, BLOCKS, PICKED], BF16, name="adjacency")
+        nc.scalar.dma_start(adjacency[:], adj_t.rearrange("(k p) i -> p k i", p=P))
         weights = held.tile([P, P], BF16, name="weights")
         nc.sync.dma_start(weights[:], w)
-        adjacency = held.tile([P, BLOCKS, PICKED], BF16, name="adjacency")
-        nc.sync.dma_start(adjacency[:], adj_t.rearrange("(k p) i -> p k i", p=P))
         bias = held.tile([P, 1], F32, name="bias")
         nc.sync.dma_start(bias[:], b)
 

@@ -10,6 +10,8 @@ PICKED = 512
 BLOCKS = PICKED // P
 HALF = PICKED // 2
 
+PIECES = ((0, 2), (2, 1), (3, 1))
+
 WARM_UP = 8
 
 FLOPS = 2 * PICKED * P * P + 2 * PICKED * PICKED * P
@@ -43,12 +45,16 @@ def tile_fuselayer_kernel(tc, x, w, adj_t, b, offs, out):
             nc.tensor.matmul(unread[:], zeros[:, 0:P], zeros[:], start=True, stop=True)
 
         totals = [psum.tile([P, HALF], F32, name=f"total{h}") for h in range(2)]
+        picked_views = []
+        for piece, (first_block, blocks) in enumerate(PIECES):
+            picked = held.tile([P, blocks * P], F32, name=f"picked{piece}")
+            piece_offsets = offsets[:, first_block * (P // 16) : (first_block + blocks) * (P // 16)]
+            nc.scalar.activation(picked[:], nodes[:].indirect(piece_offsets), COPY)
+            for inner in range(blocks):
+                picked_views.append(picked[:].bitcast(BF16)[:, 2 * inner * P + 1 : 2 * (inner + 1) * P : 2])
         for k in range(BLOCKS):
-            picked = held.tile([P, P], F32, name=f"picked{k}")
-            block_offsets = offsets[:, k * (P // 16) : (k + 1) * (P // 16)]
-            nc.scalar.activation(picked[:], nodes[:].indirect(block_offsets), COPY)
-            picked_bf = picked[:].bitcast(BF16)[:, 1 : 2 * P : 2]
-            projected = psum.tile([P, P], F32, name=f"projected{k}")
+            picked_bf = picked_views[k]
+            projected = psum.tile([P, P], BF16, name=f"projected{k}")
             nc.tensor.matmul(projected[:], picked_bf, weights[:], start=True, stop=True)
             rounded = held.tile([P, P], BF16, name=f"rounded{k}")
             nc.vector.tensor_copy(rounded[:], projected[:])

@@ -34,15 +34,14 @@ def tile_fuselayer_kernel(tc, x, w, adj_t, b, offs, out):
         bias = held.tile([P, 1], F32, name="bias")
         nc.sync.dma_start(bias[:], b)
 
-        first = held.tile([P, 1], F32, name="first")
-        nc.vector.memset(first[:], 0.0)
-        nc.scalar.activation(first[:], first[:], COPY)
-
-        zeros = held.tile([P, PICKED], BF16, name="zeros")
+        zeros = held.tile([P, P], BF16, name="zeros")
         nc.vector.memset(zeros[:], 0.0)
         unread = psum.tile([P, PICKED], F32, name="unread")
         for turn in range(WARM_UP):
-            nc.tensor.matmul(unread[:], zeros[:, 0:P], zeros[:], start=True, stop=True)
+            nc.tensor.matmul(unread[:], zeros[:], zeros[:, 0:1].to_broadcast([P, PICKED]), start=True, stop=True)
+
+        first = held.tile([P, 1], F32, name="first")
+        nc.scalar.activation(first[:], zeros[:, 0:1], COPY)
 
         totals = [psum.tile([P, HALF], F32, name=f"total{h}") for h in range(2)]
         picked_views = []

@@ -8,11 +8,12 @@ P = 128
 NODES = 1024
 PICKED = 512
 BLOCKS = PICKED // P
-HALF = PICKED // 2
+FIRST = 304
+PARTS = ((0, FIRST), (FIRST, PICKED))
 
 PIECES = ((0, 2), (2, 1), (3, 1))
 
-WARM_UP = 8
+WARM_UP = 6
 
 FLOPS = 2 * PICKED * P * P + 2 * PICKED * PICKED * P
 
@@ -43,7 +44,7 @@ def tile_fuselayer_kernel(tc, x, w, adj_t, b, offs, out):
         first = held.tile([P, 1], F32, name="first")
         nc.scalar.activation(first[:], zeros[:, 0:1], COPY)
 
-        totals = [psum.tile([P, HALF], F32, name=f"total{h}") for h in range(2)]
+        totals = [psum.tile([P, stop - start], F32, name=f"total{start}") for start, stop in PARTS]
         picked_views = []
         for piece, (first_block, blocks) in enumerate(PIECES):
             picked = held.tile([P, blocks * P], F32, name=f"picked{piece}")
@@ -57,16 +58,16 @@ def tile_fuselayer_kernel(tc, x, w, adj_t, b, offs, out):
             nc.tensor.matmul(projected[:], picked_bf, weights[:], start=True, stop=True)
             rounded = held.tile([P, P], BF16, name=f"rounded{k}")
             nc.vector.tensor_copy(rounded[:], projected[:])
-            for h in range(2):
+            for total, (start, stop) in zip(totals, PARTS):
                 nc.tensor.matmul(
-                    totals[h][:],
+                    total[:],
                     rounded[:],
-                    adjacency[:, k, h * HALF : (h + 1) * HALF],
+                    adjacency[:, k, start:stop],
                     start=(k == 0),
                     stop=(k == BLOCKS - 1),
                 )
 
         result = held.tile([P, PICKED], F32, name="result")
-        nc.scalar.activation(result[:, 0:HALF], totals[0][:], RELU, bias=bias[:, 0:1])
-        nc.vector.tensor_scalar(result[:, HALF:PICKED], totals[1][:], bias[:, 0:1], 0.0, ADD, MAX)
+        nc.scalar.activation(result[:, 0:FIRST], totals[0][:], RELU, bias=bias[:, 0:1])
+        nc.vector.tensor_scalar(result[:, FIRST:PICKED], totals[1][:], bias[:, 0:1], 0.0, ADD, MAX)
         nc.sync.dma_start(out, result[:])

import concourse.mybir as mybir

F32, BF16, U16 = mybir.dt.float32, mybir.dt.bfloat16, mybir.dt.uint16
COPY, RELU = mybir.ActivationFunctionType.Copy, mybir.ActivationFunctionType.Relu
ADD, MAX = mybir.AluOpType.add, mybir.AluOpType.max

P = 128
NODES = 1024
PICKED = 512
BLOCKS = PICKED // P
FIRST = 304
PARTS = ((0, FIRST), (FIRST, PICKED))

PIECES = ((0, 2), (2, 1), (3, 1))

WARM_UP = 6

FLOPS = 2 * PICKED * P * P + 2 * PICKED * PICKED * P


def tile_fuselayer_kernel(tc, x, w, adj_t, b, offs, out):
    nc = tc.nc
    with (
        tc.tile_pool(name="held", bufs=1) as held,
        tc.psum_pool(name="psum", bufs=1) as psum,
    ):
        nodes = held.tile([P, NODES], F32, name="nodes")
        nc.scalar.dma_start(nodes[:], x)
        offsets = held.tile([P, PICKED // 16], U16, name="offsets")
        nc.sync.dma_start(offsets[:], offs)
        adjacency = held.tile([P, BLOCKS, PICKED], BF16, name="adjacency")
        nc.scalar.dma_start(adjacency[:], adj_t.rearrange("(k p) i -> p k i", p=P))
        weights = held.tile([P, P], BF16, name="weights")
        nc.sync.dma_start(weights[:], w)
        bias = held.tile([P, 1], F32, name="bias")
        nc.sync.dma_start(bias[:], b)

        zeros = held.tile([P, P], BF16, name="zeros")
        nc.vector.memset(zeros[:], 0.0)
        unread = psum.tile([P, PICKED], F32, name="unread")
        for turn in range(WARM_UP):
            nc.tensor.matmul(unread[:], zeros[:], zeros[:, 0:1].to_broadcast([P, PICKED]), start=True, stop=True)

        first = held.tile([P, 1], F32, name="first")
        nc.scalar.activation(first[:], zeros[:, 0:1], COPY)

        totals = [psum.tile([P, stop - start], F32, name=f"total{start}") for start, stop in PARTS]
        picked_views = []
        for piece, (first_block, blocks) in enumerate(PIECES):
            picked = held.tile([P, blocks * P], F32, name=f"picked{piece}")
            piece_offsets = offsets[:, first_block * (P // 16) : (first_block + blocks) * (P // 16)]
            nc.scalar.activation(picked[:], nodes[:].indirect(piece_offsets), COPY)
            for inner in range(blocks):
                picked_views.append(picked[:].bitcast(BF16)[:, 2 * inner * P + 1 : 2 * (inner + 1) * P : 2])
        for k in range(BLOCKS):
            picked_bf = picked_views[k]
            projected = psum.tile([P, P], BF16, name=f"projected{k}")
            nc.tensor.matmul(projected[:], picked_bf, weights[:], start=True, stop=True)
            rounded = held.tile([P, P], BF16, name=f"rounded{k}")
            nc.vector.tensor_copy(rounded[:], projected[:])
            for total, (start, stop) in zip(totals, PARTS):
                nc.tensor.matmul(
                    total[:],
                    rounded[:],
                    adjacency[:, k, start:stop],
                    start=(k == 0),
                    stop=(k == BLOCKS - 1),
                )

        result = held.tile([P, PICKED], F32, name="result")
        nc.scalar.activation(result[:, 0:FIRST], totals[0][:], RELU, bias=bias[:, 0:1])
        nc.vector.tensor_scalar(result[:, FIRST:PICKED], totals[1][:], bias[:, 0:1], 0.0, ADD, MAX)
        nc.sync.dma_start(out, result[:])
